import numpy as np
import ml_dtypes

BF16 = ml_dtypes.bfloat16


def bf(x):
    return np.asarray(x, np.float32).astype(BF16)


def f32(x):
    return np.asarray(x, np.float32)


def f64(x):
    return np.asarray(x).astype(np.float64)


def striped(idx):
    return np.tile(idx.reshape(-1, 16).T, (8, 1))


D, HD, S, M, N = 128, 32, 1024, 512, 512
SCALING = (HD / 3.0) ** 0.5 / HD
SMOOTH = 20.0


def setup_inputs():
    return {"kt": bf(np.random.standard_normal((D, S))), "qt": bf(np.random.standard_normal((D, M))), "attn_bias": f32(np.random.standard_normal((M, N))), "law": f32(0.5 + 0.5 * np.random.random((M, N))), "offs": striped(np.random.permutation(np.tile(np.arange(S), 2))[:N])}


def reference(kt, qt, attn_bias, law, offs):
    idx = offs[:16].T.reshape(-1)
    aw = SCALING * (f64(qt).T @ f64(kt)[:, idx]) + f64(attn_bias)
    return (aw + SMOOTH) * f64(law) - SMOOTH

@@ -1,0 +1,49 @@
+import math
+
+import concourse.mybir as mybir
+
+BF16, F32, U16 = mybir.dt.bfloat16, mybir.dt.float32, mybir.dt.uint16
+MULT, ADD = mybir.AluOpType.mult, mybir.AluOpType.add
+COPY = mybir.ActivationFunctionType.Copy
+
+P = 128
+S = 1024
+M = 512
+N = 512
+SC = math.sqrt(32.0 / 3.0) / 32.0
+SMOOTH = 20.0
+FLOPS = 2 * P * M * N
+
+
+def tile_encoderlayer_kernel(tc, kt, qt, attn_bias, law, offs, out):
+    nc = tc.nc
+    blocks = M // P
+    with (
+        tc.tile_pool(name="held", bufs=1) as held,
+        tc.tile_pool(name="work", bufs=blocks) as work,
+        tc.psum_pool(name="psum", bufs=blocks) as psum,
+    ):
+        offsets = held.tile([P, N // 16], U16, name="offsets")
+        nc.sync.dma_start(offsets[:], offs)
+        keys = held.tile([P, S], BF16, name="keys")
+        nc.sync.dma_start(keys[:], kt)
+        queries = held.tile([P, M], BF16, name="queries")
+        nc.sync.dma_start(queries[:], qt)
+
+        for b in range(blocks):
+            rows = slice(b * P, (b + 1) * P)
+            bias_b = work.tile([P, N], F32, name="bias_b")
+            nc.sync.dma_start(bias_b[:], attn_bias[rows, :])
+            law_b = work.tile([P, N], F32, name="law_b")
+            nc.sync.dma_start(law_b[:], law[rows, :])
+
+            product = psum.tile([P, N], F32, name="product")
+            nc.tensor.matmul(product[:], queries[:, rows], keys[:].indirect(offsets[:]), start=True, stop=True)
+
+            logits = work.tile([P, N], F32, name="logits")
+            nc.vector.scalar_tensor_tensor(logits[:], product[:], SC, bias_b[:], MULT, ADD)
+            weighted = work.tile([P, N], F32, name="weighted")
+            nc.vector.scalar_tensor_tensor(weighted[:], logits[:], SMOOTH, law_b[:], ADD, MULT)
+            result = work.tile([P, N], F32, name="result")
+            nc.scalar.activation(result[:], weighted[:], COPY, bias=-SMOOTH, scale=1.0)
+            nc.scalar.dma_start(out[rows, :], result[:])

@@ -28,14 +28,14 @@ def tile_encoderlayer_kernel(tc, kt, qt, attn_bias, law, offs, out):
         keys = held.tile([P, S], BF16, name="keys")
         nc.sync.dma_start(keys[:], kt)
         queries = held.tile([P, M], BF16, name="queries")
-        nc.sync.dma_start(queries[:], qt)
+        nc.scalar.dma_start(queries[:], qt)
 
         for b in range(blocks):
             rows = slice(b * P, (b + 1) * P)
             bias_b = work.tile([P, N], F32, name="bias_b")
             nc.sync.dma_start(bias_b[:], attn_bias[rows, :])
             law_b = work.tile([P, N], F32, name="law_b")
-            nc.sync.dma_start(law_b[:], law[rows, :])
+            nc.scalar.dma_start(law_b[:], law[rows, :])
 
             product = psum.tile([P, N], F32, name="product")
             nc.tensor.matmul(product[:], queries[:, rows], keys[:].indirect(offsets[:]), start=True, stop=True)

@@ -15,12 +15,15 @@ SMOOTH = 20.0
 FLOPS = 2 * P * M * N
 
 
+LAST_CUT = 2
+
+
 def tile_encoderlayer_kernel(tc, kt, qt, attn_bias, law, offs, out):
     nc = tc.nc
     blocks = M // P
     with (
         tc.tile_pool(name="held", bufs=1) as held,
-        tc.tile_pool(name="work", bufs=blocks) as work,
+        tc.tile_pool(name="work", bufs=blocks - 1 + LAST_CUT) as work,
         tc.psum_pool(name="psum", bufs=blocks) as psum,
     ):
         offsets = held.tile([P, N // 16], U16, name="offsets")
@@ -28,22 +31,26 @@ def tile_encoderlayer_kernel(tc, kt, qt, attn_bias, law, offs, out):
         keys = held.tile([P, S], BF16, name="keys")
         nc.sync.dma_start(keys[:], kt)
         queries = held.tile([P, M], BF16, name="queries")
-        nc.scalar.dma_start(queries[:], qt)
+        nc.sync.dma_start(queries[:], qt)
 
         for b in range(blocks):
             rows = slice(b * P, (b + 1) * P)
-            bias_b = work.tile([P, N], F32, name="bias_b")
-            nc.sync.dma_start(bias_b[:], attn_bias[rows, :])
-            law_b = work.tile([P, N], F32, name="law_b")
-            nc.scalar.dma_start(law_b[:], law[rows, :])
-
             product = psum.tile([P, N], F32, name="product")
             nc.tensor.matmul(product[:], queries[:, rows], keys[:].indirect(offsets[:]), start=True, stop=True)
 
-            logits = work.tile([P, N], F32, name="logits")
-            nc.vector.scalar_tensor_tensor(logits[:], product[:], SC, bias_b[:], MULT, ADD)
-            weighted = work.tile([P, N], F32, name="weighted")
-            nc.vector.scalar_tensor_tensor(weighted[:], logits[:], SMOOTH, law_b[:], ADD, MULT)
-            result = work.tile([P, N], F32, name="result")
-            nc.scalar.activation(result[:], weighted[:], COPY, bias=-SMOOTH, scale=1.0)
-            nc.scalar.dma_start(out[rows, :], result[:])
+            pieces = LAST_CUT if b == blocks - 1 else 1
+            width = N // pieces
+            for c in range(pieces):
+                cols = slice(c * width, (c + 1) * width)
+                bias_c = work.tile([P, width], F32, name="bias_c")
+                nc.sync.dma_start(bias_c[:], attn_bias[rows, cols])
+                law_c = work.tile([P, width], F32, name="law_c")
+                nc.sync.dma_start(law_c[:], law[rows, cols])
+
+                logits = work.tile([P, width], F32, name="logits")
+                nc.vector.scalar_tensor_tensor(logits[:], product[:, cols], SC, bias_c[:], MULT, ADD)
+                weighted = work.tile([P, width], F32, name="weighted")
+                nc.vector.scalar_tensor_tensor(weighted[:], logits[:], SMOOTH, law_c[:], ADD, MULT)
+                result = work.tile([P, width], F32, name="result")
+                nc.scalar.activation(result[:], weighted[:], COPY, bias=-SMOOTH, scale=1.0)
+                nc.scalar.dma_start(out[rows, cols], result[:])

@@ -23,6 +23,7 @@ def tile_encoderlayer_kernel(tc, kt, qt, attn_bias, law, offs, out):
     blocks = M // P
     with (
         tc.tile_pool(name="held", bufs=1) as held,
+        tc.tile_pool(name="loaded", bufs=blocks) as loaded,
         tc.tile_pool(name="work", bufs=blocks - 1 + LAST_CUT) as work,
         tc.psum_pool(name="psum", bufs=blocks) as psum,
     ):
@@ -35,6 +36,11 @@ def tile_encoderlayer_kernel(tc, kt, qt, attn_bias, law, offs, out):
 
         for b in range(blocks):
             rows = slice(b * P, (b + 1) * P)
+            bias_b = loaded.tile([P, N], F32, name="bias_b")
+            nc.sync.dma_start(bias_b[:], attn_bias[rows, :])
+            law_b = loaded.tile([P, N], F32, name="law_b")
+            nc.sync.dma_start(law_b[:], law[rows, :])
+
             product = psum.tile([P, N], F32, name="product")
             nc.tensor.matmul(product[:], queries[:, rows], keys[:].indirect(offsets[:]), start=True, stop=True)
 
@@ -42,15 +48,10 @@ def tile_encoderlayer_kernel(tc, kt, qt, attn_bias, law, offs, out):
             width = N // pieces
             for c in range(pieces):
                 cols = slice(c * width, (c + 1) * width)
-                bias_c = work.tile([P, width], F32, name="bias_c")
-                nc.sync.dma_start(bias_c[:], attn_bias[rows, cols])
-                law_c = work.tile([P, width], F32, name="law_c")
-                nc.sync.dma_start(law_c[:], law[rows, cols])
-
                 logits = work.tile([P, width], F32, name="logits")
-                nc.vector.scalar_tensor_tensor(logits[:], product[:, cols], SC, bias_c[:], MULT, ADD)
+                nc.vector.scalar_tensor_tensor(logits[:], product[:, cols], SC, bias_b[:, cols], MULT, ADD)
                 weighted = work.tile([P, width], F32, name="weighted")
-                nc.vector.scalar_tensor_tensor(weighted[:], logits[:], SMOOTH, law_c[:], ADD, MULT)
+                nc.vector.scalar_tensor_tensor(weighted[:], logits[:], SMOOTH, law_b[:, cols], ADD, MULT)
                 result = work.tile([P, width], F32, name="result")
                 nc.scalar.activation(result[:], weighted[:], COPY, bias=-SMOOTH, scale=1.0)
-                nc.scalar.dma_start(out[rows, cols], result[:])
+                nc.sync.dma_start(out[rows, cols], result[:])

@@ -7,6 +7,7 @@ MULT, ADD = mybir.AluOpType.mult, mybir.AluOpType.add
 COPY = mybir.ActivationFunctionType.Copy
 
 P = 128
+BLOCKS = 4
 S = 1024
 M = 512
 N = 512
@@ -14,44 +15,51 @@ SC = math.sqrt(32.0 / 3.0) / 32.0
 SMOOTH = 20.0
 FLOPS = 2 * P * M * N
 
-
-LAST_CUT = 2
+WIDE = BLOCKS * N
+LOADS = ((0, 512), (512, 1536), (1536, 2048))
+PIECES = ((0, 512), (512, 1024), (1024, 1536), (1536, 1792), (1792, 2048))
+STORES = ((0, 1024), (1024, 1536), (1536, 1792), (1792, 2048))
 
 
 def tile_encoderlayer_kernel(tc, kt, qt, attn_bias, law, offs, out):
     nc = tc.nc
-    blocks = M // P
+    bias_wide = attn_bias.rearrange("(p b) j -> p (b j)", b=BLOCKS)
+    law_wide = law.rearrange("(p b) j -> p (b j)", b=BLOCKS)
+    out_wide = out.rearrange("(p b) j -> p (b j)", b=BLOCKS)
     with (
         tc.tile_pool(name="held", bufs=1) as held,
-        tc.tile_pool(name="loaded", bufs=blocks) as loaded,
-        tc.tile_pool(name="work", bufs=blocks - 1 + LAST_CUT) as work,
-        tc.psum_pool(name="psum", bufs=blocks) as psum,
+        tc.tile_pool(name="work", bufs=len(PIECES)) as work,
+        tc.psum_pool(name="psum", bufs=BLOCKS) as psum,
     ):
         offsets = held.tile([P, N // 16], U16, name="offsets")
         nc.sync.dma_start(offsets[:], offs)
-        keys = held.tile([P, S], BF16, name="keys")
-        nc.sync.dma_start(keys[:], kt)
         queries = held.tile([P, M], BF16, name="queries")
         nc.sync.dma_start(queries[:], qt)
+        keys = held.tile([P, S], BF16, name="keys")
+        nc.sync.dma_start(keys[:], kt)
+        biases = held.tile([P, WIDE], F32, name="biases")
+        laws = held.tile([P, WIDE], F32, name="laws")
+        for first, end in LOADS:
+            nc.sync.dma_start(biases[:, first:end], bias_wide[:, first:end])
+            nc.sync.dma_start(laws[:, first:end], law_wide[:, first:end])
 
-        for b in range(blocks):
-            rows = slice(b * P, (b + 1) * P)
-            bias_b = loaded.tile([P, N], F32, name="bias_b")
-            nc.sync.dma_start(bias_b[:], attn_bias[rows, :])
-            law_b = loaded.tile([P, N], F32, name="law_b")
-            nc.sync.dma_start(law_b[:], law[rows, :])
+        sorted_queries = held.tile([P, BLOCKS, P], BF16, name="sorted_queries")
+        nc.vector.tensor_copy(sorted_queries[:], queries[:].rearrange("d (p b) -> d b p", b=BLOCKS))
 
+        products = []
+        for b in range(BLOCKS):
             product = psum.tile([P, N], F32, name="product")
-            nc.tensor.matmul(product[:], queries[:, rows], keys[:].indirect(offsets[:]), start=True, stop=True)
+            nc.tensor.matmul(product[:], sorted_queries[:, b, :], keys[:].indirect(offsets[:]), start=True, stop=True)
+            products.append(product)
 
-            pieces = LAST_CUT if b == blocks - 1 else 1
-            width = N // pieces
-            for c in range(pieces):
-                cols = slice(c * width, (c + 1) * width)
-                logits = work.tile([P, width], F32, name="logits")
-                nc.vector.scalar_tensor_tensor(logits[:], product[:, cols], SC, bias_b[:, cols], MULT, ADD)
-                weighted = work.tile([P, width], F32, name="weighted")
-                nc.vector.scalar_tensor_tensor(weighted[:], logits[:], SMOOTH, law_b[:, cols], ADD, MULT)
-                result = work.tile([P, width], F32, name="result")
-                nc.scalar.activation(result[:], weighted[:], COPY, bias=-SMOOTH, scale=1.0)
-                nc.sync.dma_start(out[rows, cols], result[:])
+        results = held.tile([P, WIDE], F32, name="results")
+        for first, end in PIECES:
+            in_block = slice(first % N, first % N + end - first)
+            logits = work.tile([P, end - first], F32, name="logits")
+            nc.vector.scalar_tensor_tensor(logits[:], products[first // N][:, in_block], SC, biases[:, first:end], MULT, ADD)
+            weighted = work.tile([P, end - first], F32, name="weighted")
+            nc.vector.scalar_tensor_tensor(weighted[:], logits[:], SMOOTH, laws[:, first:end], ADD, MULT)
+            nc.scalar.activation(results[:, first:end], weighted[:], COPY, bias=-SMOOTH, scale=1.0)
+            for store_first, store_end in STORES:
+                if store_end == end:
+                    nc.sync.dma_start(out_wide[:, store_first:store_end], results[:, store_first:store_end])

@@ -18,7 +18,6 @@ FLOPS = 2 * P * M * N
 WIDE = BLOCKS * N
 LOADS = ((0, 512), (512, 1536), (1536, 2048))
 PIECES = ((0, 512), (512, 1024), (1024, 1536), (1536, 1792), (1792, 2048))
-STORES = ((0, 1024), (1024, 1536), (1536, 1792), (1792, 2048))
 
 
 def tile_encoderlayer_kernel(tc, kt, qt, attn_bias, law, offs, out):
@@ -52,14 +51,12 @@ def tile_encoderlayer_kernel(tc, kt, qt, attn_bias, law, offs, out):
             nc.tensor.matmul(product[:], sorted_queries[:, b, :], keys[:].indirect(offsets[:]), start=True, stop=True)
             products.append(product)
 
-        results = held.tile([P, WIDE], F32, name="results")
         for first, end in PIECES:
             in_block = slice(first % N, first % N + end - first)
             logits = work.tile([P, end - first], F32, name="logits")
             nc.vector.scalar_tensor_tensor(logits[:], products[first // N][:, in_block], SC, biases[:, first:end], MULT, ADD)
             weighted = work.tile([P, end - first], F32, name="weighted")
             nc.vector.scalar_tensor_tensor(weighted[:], logits[:], SMOOTH, laws[:, first:end], ADD, MULT)
-            nc.scalar.activation(results[:, first:end], weighted[:], COPY, bias=-SMOOTH, scale=1.0)
-            for store_first, store_end in STORES:
-                if store_end == end:
-                    nc.sync.dma_start(out_wide[:, store_first:store_end], results[:, store_first:store_end])
+            result = work.tile([P, end - first], F32, name="result")
+            nc.scalar.activation(result[:], weighted[:], COPY, bias=-SMOOTH, scale=1.0)
+            nc.sync.dma_start(out_wide[:, first:end], result[:])

@@ -15,16 +15,15 @@ SC = math.sqrt(32.0 / 3.0) / 32.0
 SMOOTH = 20.0
 FLOPS = 2 * P * M * N
 
-WIDE = BLOCKS * N
-LOADS = ((0, 512), (512, 1536), (1536, 2048))
-PIECES = ((0, 512), (512, 1024), (1024, 1536), (1536, 1792), (1792, 2048))
+LOADS = ((0, 1), (1, 3), (3, 4))
+PIECES = ((0, 0, 512), (1, 0, 512), (2, 0, 512), (3, 0, 256), (3, 256, 512))
 
 
 def tile_encoderlayer_kernel(tc, kt, qt, attn_bias, law, offs, out):
     nc = tc.nc
-    bias_wide = attn_bias.rearrange("(p b) j -> p (b j)", b=BLOCKS)
-    law_wide = law.rearrange("(p b) j -> p (b j)", b=BLOCKS)
-    out_wide = out.rearrange("(p b) j -> p (b j)", b=BLOCKS)
+    bias_blocks = attn_bias.rearrange("(b p) j -> p b j", p=P)
+    law_blocks = law.rearrange("(b p) j -> p b j", p=P)
+    out_blocks = out.rearrange("(b p) j -> p b j", p=P)
     with (
         tc.tile_pool(name="held", bufs=1) as held,
         tc.tile_pool(name="work", bufs=len(PIECES)) as work,
@@ -32,31 +31,30 @@ def tile_encoderlayer_kernel(tc, kt, qt, attn_bias, law, offs, out):
     ):
         offsets = held.tile([P, N // 16], U16, name="offsets")
         nc.sync.dma_start(offsets[:], offs)
-        queries = held.tile([P, M], BF16, name="queries")
-        nc.sync.dma_start(queries[:], qt)
+        first_queries = held.tile([P, P], BF16, name="first_queries")
+        nc.sync.dma_start(first_queries[:], qt[:, 0:P])
         keys = held.tile([P, S], BF16, name="keys")
         nc.sync.dma_start(keys[:], kt)
-        biases = held.tile([P, WIDE], F32, name="biases")
-        laws = held.tile([P, WIDE], F32, name="laws")
+        other_queries = held.tile([P, M - P], BF16, name="other_queries")
+        nc.sync.dma_start(other_queries[:], qt[:, P:M])
+        biases = held.tile([P, BLOCKS, N], F32, name="biases")
+        laws = held.tile([P, BLOCKS, N], F32, name="laws")
         for first, end in LOADS:
-            nc.sync.dma_start(biases[:, first:end], bias_wide[:, first:end])
-            nc.sync.dma_start(laws[:, first:end], law_wide[:, first:end])
-
-        sorted_queries = held.tile([P, BLOCKS, P], BF16, name="sorted_queries")
-        nc.vector.tensor_copy(sorted_queries[:], queries[:].rearrange("d (p b) -> d b p", b=BLOCKS))
+            nc.sync.dma_start(biases[:, first:end, :], bias_blocks[:, first:end, :])
+            nc.sync.dma_start(laws[:, first:end, :], law_blocks[:, first:end, :])
 
         products = []
         for b in range(BLOCKS):
+            weights = first_queries[:] if b == 0 else other_queries[:, (b - 1) * P : b * P]
             product = psum.tile([P, N], F32, name="product")
-            nc.tensor.matmul(product[:], sorted_queries[:, b, :], keys[:].indirect(offsets[:]), start=True, stop=True)
+            nc.tensor.matmul(product[:], weights, keys[:].indirect(offsets[:]), start=True, stop=True)
             products.append(product)
 
-        for first, end in PIECES:
-            in_block = slice(first % N, first % N + end - first)
+        for b, first, end in PIECES:
             logits = work.tile([P, end - first], F32, name="logits")
-            nc.vector.scalar_tensor_tensor(logits[:], products[first // N][:, in_block], SC, biases[:, first:end], MULT, ADD)
+            nc.vector.scalar_tensor_tensor(logits[:], products[b][:, first:end], SC, biases[:, b, first:end], MULT, ADD)
             weighted = work.tile([P, end - first], F32, name="weighted")
-            nc.vector.scalar_tensor_tensor(weighted[:], logits[:], SMOOTH, laws[:, first:end], ADD, MULT)
+            nc.vector.scalar_tensor_tensor(weighted[:], logits[:], SMOOTH, laws[:, b, first:end], ADD, MULT)
             result = work.tile([P, end - first], F32, name="result")
             nc.scalar.activation(result[:], weighted[:], COPY, bias=-SMOOTH, scale=1.0)
-            nc.sync.dma_start(out_wide[:, first:end], result[:])
+            nc.sync.dma_start(out_blocks[:, b, first:end], result[:])

@@ -15,19 +15,17 @@ SC = math.sqrt(32.0 / 3.0) / 32.0
 SMOOTH = 20.0
 FLOPS = 2 * P * M * N
 
-LOADS = ((0, 1), (1, 3), (3, 4))
-PIECES = ((0, 0, 512), (1, 0, 512), (2, 0, 512), (3, 0, 256), (3, 256, 512))
+LOADS = (("bias", 0, 1), ("law", 0, 1), ("bias", 1, 2), ("law", 1, 2), ("bias", 2, 3), ("law", 2, 3), ("bias", 3, 4), ("law", 3, 4))
+HALF = N // 2
+LEAVES = ((0, 0, 512), (1, 0, 512), (2, 0, 512), (3, 0, 256), (3, 256, 512))
 
 
 def tile_encoderlayer_kernel(tc, kt, qt, attn_bias, law, offs, out):
     nc = tc.nc
-    bias_blocks = attn_bias.rearrange("(b p) j -> p b j", p=P)
-    law_blocks = law.rearrange("(b p) j -> p b j", p=P)
     out_blocks = out.rearrange("(b p) j -> p b j", p=P)
     with (
         tc.tile_pool(name="held", bufs=1) as held,
-        tc.tile_pool(name="work", bufs=len(PIECES)) as work,
-        tc.psum_pool(name="psum", bufs=BLOCKS) as psum,
+        tc.psum_pool(name="psum", bufs=2 * BLOCKS) as psum,
     ):
         offsets = held.tile([P, N // 16], U16, name="offsets")
         nc.sync.dma_start(offsets[:], offs)
@@ -39,22 +37,25 @@ def tile_encoderlayer_kernel(tc, kt, qt, attn_bias, law, offs, out):
         nc.sync.dma_start(other_queries[:], qt[:, P:M])
         biases = held.tile([P, BLOCKS, N], F32, name="biases")
         laws = held.tile([P, BLOCKS, N], F32, name="laws")
-        for first, end in LOADS:
-            nc.sync.dma_start(biases[:, first:end, :], bias_blocks[:, first:end, :])
-            nc.sync.dma_start(laws[:, first:end, :], law_blocks[:, first:end, :])
+        tiles = {"bias": biases, "law": laws}
+        arrays = {"bias": attn_bias.rearrange("(b p) j -> p b j", p=P), "law": law.rearrange("(b p) j -> p b j", p=P)}
+        for name, first, end in LOADS:
+            nc.sync.dma_start(tiles[name][:, first:end, :], arrays[name][:, first:end, :])
+        logits = held.tile([P, BLOCKS, N], F32, name="logits")
+        weighted = held.tile([P, BLOCKS, N], F32, name="weighted")
+        result = held.tile([P, BLOCKS, N], F32, name="result")
 
-        products = []
         for b in range(BLOCKS):
             weights = first_queries[:] if b == 0 else other_queries[:, (b - 1) * P : b * P]
-            product = psum.tile([P, N], F32, name="product")
-            nc.tensor.matmul(product[:], weights, keys[:].indirect(offsets[:]), start=True, stop=True)
-            products.append(product)
+            for first in (0, HALF):
+                end = first + HALF
+                product = psum.tile([P, HALF], F32, name="product")
+                nc.tensor.matmul(product[:], weights, keys[:].indirect(offsets[:, first // 16 : end // 16]), start=True, stop=True)
+                nc.vector.scalar_tensor_tensor(logits[:, b, first:end], product[:], SC, biases[:, b, first:end], MULT, ADD)
+            for first in (0, HALF):
+                end = first + HALF
+                nc.vector.scalar_tensor_tensor(weighted[:, b, first:end], logits[:, b, first:end], SMOOTH, laws[:, b, first:end], ADD, MULT)
 
-        for b, first, end in PIECES:
-            logits = work.tile([P, end - first], F32, name="logits")
-            nc.vector.scalar_tensor_tensor(logits[:], products[b][:, first:end], SC, biases[:, b, first:end], MULT, ADD)
-            weighted = work.tile([P, end - first], F32, name="weighted")
-            nc.vector.scalar_tensor_tensor(weighted[:], logits[:], SMOOTH, laws[:, b, first:end], ADD, MULT)
-            result = work.tile([P, end - first], F32, name="result")
-            nc.scalar.activation(result[:], weighted[:], COPY, bias=-SMOOTH, scale=1.0)
-            nc.sync.dma_start(out_blocks[:, b, first:end], result[:])
+        for b, first, end in LEAVES:
+            nc.scalar.activation(result[:, b, first:end], weighted[:, b, first:end], COPY, bias=-SMOOTH, scale=1.0)
+            nc.sync.dma_start(out_blocks[:, b, first:end], result[:, b, first:end])

@@ -29,12 +29,10 @@ def tile_encoderlayer_kernel(tc, kt, qt, attn_bias, law, offs, out):
     ):
         offsets = held.tile([P, N // 16], U16, name="offsets")
         nc.sync.dma_start(offsets[:], offs)
-        first_queries = held.tile([P, P], BF16, name="first_queries")
-        nc.sync.dma_start(first_queries[:], qt[:, 0:P])
+        queries = held.tile([P, M], BF16, name="queries")
+        nc.sync.dma_start(queries[:], qt)
         keys = held.tile([P, S], BF16, name="keys")
         nc.sync.dma_start(keys[:], kt)
-        other_queries = held.tile([P, M - P], BF16, name="other_queries")
-        nc.sync.dma_start(other_queries[:], qt[:, P:M])
         biases = held.tile([P, BLOCKS, N], F32, name="biases")
         laws = held.tile([P, BLOCKS, N], F32, name="laws")
         tiles = {"bias": biases, "law": laws}
@@ -46,7 +44,7 @@ def tile_encoderlayer_kernel(tc, kt, qt, attn_bias, law, offs, out):
         result = held.tile([P, BLOCKS, N], F32, name="result")
 
         for b in range(BLOCKS):
-            weights = first_queries[:] if b == 0 else other_queries[:, (b - 1) * P : b * P]
+            weights = queries[:, b * P : (b + 1) * P]
             for first in (0, HALF):
                 end = first + HALF
                 product = psum.tile([P, HALF], F32, name="product")

@@ -15,9 +15,14 @@ SC = math.sqrt(32.0 / 3.0) / 32.0
 SMOOTH = 20.0
 FLOPS = 2 * P * M * N
 
-LOADS = (("bias", 0, 1), ("law", 0, 1), ("bias", 1, 2), ("law", 1, 2), ("bias", 2, 3), ("law", 2, 3), ("bias", 3, 4), ("law", 3, 4))
 HALF = N // 2
+LOADS = (
+    ("bias", 0, 0, 512), ("law", 0, 0, 512), ("bias", 1, 0, 512), ("law", 1, 0, 512),
+    ("bias", 2, 0, 512), ("law", 2, 0, 512), ("bias", 3, 0, 512), ("law", 3, 0, 256), ("law", 3, 256, 512),
+)
+LOOKUPS = ((0, 0, 256), (0, 256, 512), (1, 0, 256), (1, 256, 512), (2, 0, 256), (2, 256, 512), (3, 0, 256), (3, 256, 512))
 LEAVES = ((0, 0, 512), (1, 0, 512), (2, 0, 512), (3, 0, 256), (3, 256, 512))
+STORES = {(1, 0, 512): (0, 2, 0, 512), (2, 0, 512): (2, 3, 0, 512), (3, 0, 256): (3, 4, 0, 256), (3, 256, 512): (3, 4, 256, 512)}
 
 
 def tile_encoderlayer_kernel(tc, kt, qt, attn_bias, law, offs, out):
@@ -25,7 +30,7 @@ def tile_encoderlayer_kernel(tc, kt, qt, attn_bias, law, offs, out):
     out_blocks = out.rearrange("(b p) j -> p b j", p=P)
     with (
         tc.tile_pool(name="held", bufs=1) as held,
-        tc.psum_pool(name="psum", bufs=2 * BLOCKS) as psum,
+        tc.psum_pool(name="psum", bufs=len(LOOKUPS)) as psum,
     ):
         offsets = held.tile([P, N // 16], U16, name="offsets")
         nc.sync.dma_start(offsets[:], offs)
@@ -37,23 +42,30 @@ def tile_encoderlayer_kernel(tc, kt, qt, attn_bias, law, offs, out):
         laws = held.tile([P, BLOCKS, N], F32, name="laws")
         tiles = {"bias": biases, "law": laws}
         arrays = {"bias": attn_bias.rearrange("(b p) j -> p b j", p=P), "law": law.rearrange("(b p) j -> p b j", p=P)}
-        for name, first, end in LOADS:
-            nc.sync.dma_start(tiles[name][:, first:end, :], arrays[name][:, first:end, :])
+        for name, b, first, end in LOADS:
+            nc.sync.dma_start(tiles[name][:, b, first:end], arrays[name][:, b, first:end])
         logits = held.tile([P, BLOCKS, N], F32, name="logits")
         weighted = held.tile([P, BLOCKS, N], F32, name="weighted")
         result = held.tile([P, BLOCKS, N], F32, name="result")
 
+        products = {}
+        for b, first, end in LOOKUPS:
+            product = psum.tile([P, end - first], F32, name="product")
+            nc.tensor.matmul(product[:], queries[:, b * P : (b + 1) * P], keys[:].indirect(offsets[:, first // 16 : end // 16]), start=True, stop=True)
+            for half in range(first, end, HALF):
+                products[(b, half)] = product[:, half - first : half - first + HALF]
+
         for b in range(BLOCKS):
-            weights = queries[:, b * P : (b + 1) * P]
             for first in (0, HALF):
                 end = first + HALF
-                product = psum.tile([P, HALF], F32, name="product")
-                nc.tensor.matmul(product[:], weights, keys[:].indirect(offsets[:, first // 16 : end // 16]), start=True, stop=True)
-                nc.vector.scalar_tensor_tensor(logits[:, b, first:end], product[:], SC, biases[:, b, first:end], MULT, ADD)
+                nc.vector.scalar_tensor_tensor(logits[:, b, first:end], products[(b, first)], SC, biases[:, b, first:end], MULT, ADD)
             for first in (0, HALF):
                 end = first + HALF
                 nc.vector.scalar_tensor_tensor(weighted[:, b, first:end], logits[:, b, first:end], SMOOTH, laws[:, b, first:end], ADD, MULT)
 
-        for b, first, end in LEAVES:
+        for leaf in LEAVES:
+            b, first, end = leaf
             nc.scalar.activation(result[:, b, first:end], weighted[:, b, first:end], COPY, bias=-SMOOTH, scale=1.0)
-            nc.sync.dma_start(out_blocks[:, b, first:end], result[:, b, first:end])
+            if leaf in STORES:
+                b, after, first, end = STORES[leaf]
+                nc.sync.dma_start(out_blocks[:, b:after, first:end], result[:, b:after, first:end])

import math

import concourse.mybir as mybir

BF16, F32, U16 = mybir.dt.bfloat16, mybir.dt.float32, mybir.dt.uint16
MULT, ADD = mybir.AluOpType.mult, mybir.AluOpType.add
COPY = mybir.ActivationFunctionType.Copy

P = 128
BLOCKS = 4
S = 1024
M = 512
N = 512
SC = math.sqrt(32.0 / 3.0) / 32.0
SMOOTH = 20.0
FLOPS = 2 * P * M * N

HALF = N // 2
LOADS = (
    ("bias", 0, 0, 512), ("law", 0, 0, 512), ("bias", 1, 0, 512), ("law", 1, 0, 512),
    ("bias", 2, 0, 512), ("law", 2, 0, 512), ("bias", 3, 0, 512), ("law", 3, 0, 256), ("law", 3, 256, 512),
)
LOOKUPS = ((0, 0, 256), (0, 256, 512), (1, 0, 256), (1, 256, 512), (2, 0, 256), (2, 256, 512), (3, 0, 256), (3, 256, 512))
LEAVES = ((0, 0, 512), (1, 0, 512), (2, 0, 512), (3, 0, 256), (3, 256, 512))
STORES = {(1, 0, 512): (0, 2, 0, 512), (2, 0, 512): (2, 3, 0, 512), (3, 0, 256): (3, 4, 0, 256), (3, 256, 512): (3, 4, 256, 512)}


def tile_encoderlayer_kernel(tc, kt, qt, attn_bias, law, offs, out):
    nc = tc.nc
    out_blocks = out.rearrange("(b p) j -> p b j", p=P)
    with (
        tc.tile_pool(name="held", bufs=1) as held,
        tc.psum_pool(name="psum", bufs=len(LOOKUPS)) as psum,
    ):
        offsets = held.tile([P, N // 16], U16, name="offsets")
        nc.sync.dma_start(offsets[:], offs)
        queries = held.tile([P, M], BF16, name="queries")
        nc.sync.dma_start(queries[:], qt)
        keys = held.tile([P, S], BF16, name="keys")
        nc.sync.dma_start(keys[:], kt)
        biases = held.tile([P, BLOCKS, N], F32, name="biases")
        laws = held.tile([P, BLOCKS, N], F32, name="laws")
        tiles = {"bias": biases, "law": laws}
        arrays = {"bias": attn_bias.rearrange("(b p) j -> p b j", p=P), "law": law.rearrange("(b p) j -> p b j", p=P)}
        for name, b, first, end in LOADS:
            nc.sync.dma_start(tiles[name][:, b, first:end], arrays[name][:, b, first:end])
        logits = held.tile([P, BLOCKS, N], F32, name="logits")
        weighted = held.tile([P, BLOCKS, N], F32, name="weighted")
        result = held.tile([P, BLOCKS, N], F32, name="result")

        products = {}
        for b, first, end in LOOKUPS:
            product = psum.tile([P, end - first], F32, name="product")
            nc.tensor.matmul(product[:], queries[:, b * P : (b + 1) * P], keys[:].indirect(offsets[:, first // 16 : end // 16]), start=True, stop=True)
            for half in range(first, end, HALF):
                products[(b, half)] = product[:, half - first : half - first + HALF]

        for b in range(BLOCKS):
            for first in (0, HALF):
                end = first + HALF
                nc.vector.scalar_tensor_tensor(logits[:, b, first:end], products[(b, first)], SC, biases[:, b, first:end], MULT, ADD)
            for first in (0, HALF):
                end = first + HALF
                nc.vector.scalar_tensor_tensor(weighted[:, b, first:end], logits[:, b, first:end], SMOOTH, laws[:, b, first:end], ADD, MULT)

        for leaf in LEAVES:
            b, first, end = leaf
            nc.scalar.activation(result[:, b, first:end], weighted[:, b, first:end], COPY, bias=-SMOOTH, scale=1.0)
            if leaf in STORES:
                b, after, first, end = STORES[leaf]
                nc.sync.dma_start(out_blocks[:, b:after, first:end], result[:, b:after, first:end])
